import numpy as np
import ml_dtypes


def mxq(x, axis, fmt="e4m3"):
    dtype, down = {"e4m3": (ml_dtypes.float8_e4m3fn, 7), "e5m2": (ml_dtypes.float8_e5m2, 14)}[fmt]
    v = np.moveaxis(np.asarray(x, np.float32).astype(ml_dtypes.bfloat16).astype(np.float64), axis, -1)
    blocks = v.reshape(v.shape[:-1] + (-1, 32))
    amax = np.abs(blocks).max(-1, keepdims=True)
    byte = np.maximum(np.where(amax > 0, np.frexp(amax)[1] - 1 + 127, 0) - down, 1)
    scale = np.exp2(byte - 127.0)
    codes = (blocks / scale).astype(np.float32).astype(dtype).astype(np.float64)
    return np.moveaxis((codes * scale).reshape(v.shape), -1, axis)


WIDE = False


def mx_kscale(k):
    if not WIDE:
        return np.ones(k)
    levels = np.array([10, -10, 5, -5, 0])
    a = np.random.permutation(np.resize(levels, k // 512 * 4)).reshape(k // 512, 4)
    idx = np.arange(k)
    return np.exp2(a[idx // 512, idx % 128 // 32])


BF16 = ml_dtypes.bfloat16


def bf(x):
    return np.asarray(x, np.float32).astype(BF16)


def f64(x):
    return np.asarray(x).astype(np.float64)


B, T, D, H, HD, STRIDE, KB = 8, 512, 512, 4, 128, 64, 512


def setup_inputs():
    s = mx_kscale(D)
    return {"q": bf(np.random.standard_normal((B, H, T, HD)) * 1.4),
            "k": bf(np.random.standard_normal((B, H, T, HD)) * 1.4),
            "x": bf(np.random.standard_normal((B, T, D)) * s),
            "wv": bf(np.random.standard_normal((D, D)) / np.sqrt(D) / s[None, :])}


def reference(q, k, x, wv):
    q, k = f64(q), f64(k)
    v = mxq(f64(x), 2, "e4m3") @ mxq(f64(wv), 1, "e4m3").T
    vq = mxq(v.reshape(B, T, H, HD).transpose(0, 2, 1, 3), 2, "e4m3")
    blk = np.arange(T) // STRIDE
    rows = []
    for r in range(0, T, KB):
        n = r + KB
        s = q[:, :, r:n] @ k[:, :, :n].transpose(0, 1, 3, 2) * HD ** -0.5
        s = np.where(blk[None, :n] <= blk[r:n, None], s, -np.inf)
        e = np.exp(s - s.max(-1, keepdims=True))
        rows.append((mxq(e, 3, "e4m3") @ vq[:, :, :n]) / e.sum(-1, keepdims=True))
    return np.concatenate(rows, 2).transpose(0, 2, 1, 3).reshape(B, T, D)

@@ -1,0 +1,207 @@
+from contextlib import ExitStack
+
+import concourse.mybir as mybir
+from concourse.masks import make_identity
+
+BF16 = mybir.dt.bfloat16
+F32 = mybir.dt.float32
+U32 = mybir.dt.uint32
+U8 = mybir.dt.uint8
+FP8X4 = mybir.dt.float8_e4m3fn_x4
+EXP = mybir.ActivationFunctionType.Exp
+MULT = mybir.AluOpType.mult
+MIN = mybir.AluOpType.min
+
+B, T, D, H, HD = 8, 512, 512, 4, 128
+STRIDE = 64
+P = 128
+PACK = 4
+TILES = T // P
+SCALE = HD**-0.5
+MASKED = -1.0e30
+STEPS = B * H
+
+FLOPS = 2 * B * T * D * D + 2 * 2 * B * H * T * T * HD
+
+
+def tile_stridedattention_pa_t_kernel(tc, q, k, x, wv, out):
+    nc = tc.nc
+    with ExitStack() as ctx:
+        const = ctx.enter_context(tc.tile_pool(name="const", bufs=1))
+        loads = ctx.enter_context(tc.tile_pool(name="loads", bufs=B))
+        work = ctx.enter_context(tc.tile_pool(name="work", bufs=2))
+        psum = ctx.enter_context(tc.psum_pool(name="psum", bufs=1))
+
+        wv_rows = const.tile([P, TILES * D], BF16)
+        nc.sync.dma_start(
+            out=wv_rows[:].rearrange("p (a c) -> p a c", a=TILES),
+            in_=wv.rearrange("(a p) c -> p a c", p=P),
+        )
+        x_of, q_of, k_of = [], [], []
+        for b in range(B):
+            x_rows = loads.tile([P, TILES * D], BF16)
+            nc.sync.dma_start(
+                out=x_rows[:].rearrange("p (u c) -> p u c", u=2),
+                in_=x[b].rearrange("(u p e) c -> p u (e c)", u=2, e=2),
+            )
+            q_rows = loads.tile([P, H * TILES * HD], BF16)
+            nc.sync.dma_start(
+                out=q_rows[:].rearrange("p (g d) -> p g d", d=HD),
+                in_=q[b].rearrange("h (i p) d -> p (h i) d", p=P),
+            )
+            k_rows = loads.tile([P, H * TILES * HD], BF16)
+            nc.sync.dma_start(
+                out=k_rows[:].rearrange("p (g d) -> p g d", d=HD),
+                in_=k[b].rearrange("h (i p) d -> p (h i) d", p=P),
+            )
+            x_of.append(x_rows)
+            q_of.append(q_rows)
+            k_of.append(k_rows)
+
+        ident_bf = const.tile([P, P], BF16)
+        make_identity(nc, ident_bf[:])
+        ident_f32 = const.tile([P, P], F32)
+        make_identity(nc, ident_f32[:])
+        later_block = const.tile([P, STRIDE], BF16)
+        nc.vector.memset(later_block[0:STRIDE, :], MASKED)
+        nc.vector.memset(later_block[STRIDE:P, :], 0.0)
+        e_buffers = []
+        for j in range(2):
+            e_rows = const.tile([P, TILES * T], BF16, name="e_rows%d" % j)
+            nc.vector.memset(e_rows[:], 0.0)
+            e_buffers.append(e_rows)
+
+        def flip(rows, copy_out):
+            words = rows[:].bitcast(F32)
+            grouped = work.tile([P, TILES * P * PACK], BF16, align_bytes=64, tag="grouped", bufs=3)
+            grouped_words = grouped[:].bitcast(F32).rearrange("p (a r u) -> p a r u", a=TILES, u=2)
+            for half in range(2):
+                flipped = psum.tile([P, 2, 2, P], F32, tag="flipped", bufs=3)
+                for a in range(2):
+                    for u in range(2):
+                        first = ((2 * half + a) * 2 + u) * P
+                        nc.tensor.transpose(flipped[:, a, u, :], words[:, first : first + P], ident_f32[:])
+                copy_out(
+                    out=grouped_words[:, 2 * half : 2 * half + 2, :, :],
+                    in_=flipped[:].rearrange("p a u r -> p a r u"),
+                )
+            return grouped
+
+        def quantise(grouped, what, bufs):
+            width = grouped.shape[1] // PACK
+            codes = work.tile([P, width], U32, align_bytes=64, tag=what + "_codes", bufs=bufs)
+            scales = work.tile([P, width], U8, align_bytes=64, tag=what + "_scales", bufs=bufs)
+            nc.vector.quantize_mx(out=codes[:].bitcast(FP8X4), scales=scales[:], in_=grouped[:])
+            return codes, scales
+
+        def project_values(step, x_mx, w_mx):
+            h = step % H
+            v_ps = psum.tile([P, PACK, HD], F32, tag="v_ps", bufs=1)
+            for a in range(PACK):
+                nc.tensor.matmul_mx(
+                    out=v_ps[:, a, :],
+                    lhsT=x_mx[0][:, a * P : (a + 1) * P].bitcast(FP8X4),
+                    lhsT_scale=x_mx[1][:, a * P : (a + 1) * P],
+                    rhs=w_mx[0][:, h * HD : (h + 1) * HD].bitcast(FP8X4),
+                    rhs_scale=w_mx[1][:, h * HD : (h + 1) * HD],
+                    start=True,
+                    stop=True,
+                )
+            v_grouped = work.tile([P, HD * PACK], BF16, align_bytes=64, tag="v_grouped", bufs=3)
+            nc.scalar.copy(
+                out=v_grouped[:].rearrange("p (f a) -> p f a", a=PACK),
+                in_=v_ps[:].rearrange("p a f -> p f a"),
+            )
+            return v_grouped
+
+        def flip_q_and_k(step):
+            b, h = divmod(step, H)
+            qk_ps = psum.tile([P, 2 * T], BF16, tag="qk_ps", bufs=1)
+            for i in range(TILES):
+                rows = slice((h * TILES + i) * HD, (h * TILES + i + 1) * HD)
+                nc.tensor.transpose(qk_ps[:, i * P : (i + 1) * P], q_of[b][:, rows], ident_bf[:])
+                nc.tensor.transpose(qk_ps[:, T + i * P : T + (i + 1) * P], k_of[b][:, rows], ident_bf[:])
+            qk_t = work.tile([P, 2 * T], BF16, tag="qk_t", bufs=2)
+            nc.scalar.copy(out=qk_t[:], in_=qk_ps[:])
+            return qk_t
+
+        def softmax_numerators(step, qk_t):
+            e_rows = e_buffers[step % 2]
+            neg_max = work.tile([P, TILES], F32, tag="neg_max", bufs=2)
+            row_sum = work.tile([P, TILES], F32, tag="row_sum", bufs=5)
+            for i in range(TILES):
+                seen = (i + 1) * P
+                s_ps = psum.tile([P, T], F32, tag="s_ps", bufs=2)
+                nc.tensor.matmul(
+                    s_ps[:, :seen], lhsT=qk_t[:, i * P : (i + 1) * P], rhs=qk_t[:, T : T + seen],
+                    start=True, stop=False,
+                )
+                nc.tensor.matmul(
+                    s_ps[:, seen - STRIDE : seen], lhsT=ident_bf[:], rhs=later_block[:],
+                    start=False, stop=True,
+                )
+                s_neg = work.tile([P, T], F32, tag="s_neg", bufs=4)
+                nc.vector.tensor_scalar(
+                    out=s_neg[:, :seen], in0=s_ps[:, :seen], scalar1=-SCALE, scalar2=None,
+                    op0=MULT, op1=MIN, accum_out=neg_max[:, i : i + 1],
+                )
+                nc.scalar.activation(
+                    out=e_rows[:, i * T : i * T + seen], in_=s_neg[:, :seen], func=EXP,
+                    bias=neg_max[:, i : i + 1], scale=-1.0, accum_out=row_sum[:, i : i + 1],
+                )
+            return e_rows, row_sum
+
+        def attend(e_mx, v_mx):
+            o_ps = psum.tile([P, TILES, HD], F32, tag="o_ps", bufs=1)
+            for i in range(TILES):
+                nc.tensor.matmul_mx(
+                    out=o_ps[:, i, :],
+                    lhsT=e_mx[0][:, i * P : (i + 1) * P].bitcast(FP8X4),
+                    lhsT_scale=e_mx[1][:, i * P : (i + 1) * P],
+                    rhs=v_mx[0][:].bitcast(FP8X4),
+                    rhs_scale=v_mx[1][:],
+                    start=True,
+                    stop=True,
+                )
+            return o_ps
+
+        def normalise_and_store(step, o_ps, row_sum):
+            b, h = divmod(step, H)
+            inv_sum = work.tile([P, TILES], F32, tag="inv_sum", bufs=2)
+            nc.vector.reciprocal(out=inv_sum[:], in_=row_sum[:])
+            o_sb = work.tile([P, TILES, HD], F32, tag="o_sb", bufs=3)
+            nc.vector.tensor_tensor(
+                out=o_sb[:], in0=o_ps[:], in1=inv_sum[:].unsqueeze(2).to_broadcast([P, TILES, HD]), op=MULT
+            )
+            nc.sync.dma_start(
+                out=out[b].rearrange("(i p) c -> p i c", p=P)[:, :, h * HD : (h + 1) * HD], in_=o_sb[:]
+            )
+
+        w_mx = quantise(flip(wv_rows, nc.vector.tensor_copy), "w", 1)
+        x_mx = {0: quantise(flip(x_of[0], nc.vector.tensor_copy), "x", 3)}
+        v_grouped, v_mx, qk_t, e_done, e_grouped, e_mx, o_done = {}, {}, {}, {}, {}, {}, {}
+        qk_t[0] = flip_q_and_k(0)
+        for step in range(H):
+            v_grouped[step] = project_values(step, x_mx[0], w_mx)
+            v_mx[step] = quantise(v_grouped[step], "v", 8)
+        x_mx[1] = quantise(flip(x_of[1], nc.vector.tensor_copy), "x", 3)
+
+        for n in range(STEPS + 3):
+            if 1 <= n <= STEPS:
+                e_grouped[n - 1] = flip(e_done[n - 1][0], nc.scalar.copy)
+            if n >= 3:
+                normalise_and_store(n - 3, o_done[n - 3], e_done[n - 3][1])
+            if n < STEPS:
+                e_done[n] = softmax_numerators(n, qk_t[n])
+            if 1 <= n <= STEPS:
+                e_mx[n - 1] = quantise(e_grouped[n - 1], "e", 3)
+            if H <= n + 3 < STEPS:
+                v_mx[n + 3] = quantise(v_grouped[n + 3], "v", 8)
+            if n + 1 < STEPS:
+                qk_t[n + 1] = flip_q_and_k(n + 1)
+            if n % H == H - 1 and (n + 5) // H < B:
+                x_mx[(n + 5) // H] = quantise(flip(x_of[(n + 5) // H], nc.vector.tensor_copy), "x", 3)
+            if 2 <= n < STEPS + 2:
+                o_done[n - 2] = attend(e_mx[n - 2], v_mx[n - 2])
+            if n + 4 < STEPS:
+                v_grouped[n + 4] = project_values(n + 4, x_mx[(n + 4) // H], w_mx)

@@ -20,6 +20,8 @@ TILES = T // P
 SCALE = HD**-0.5
 MASKED = -1.0e30
 STEPS = B * H
+SEEN = [(i + 1) * P for i in range(TILES)]
+FIRST = [sum(SEEN[:i]) for i in range(TILES)]
 
 FLOPS = 2 * B * T * D * D + 2 * 2 * B * H * T * T * HD
 
@@ -28,22 +30,14 @@ def tile_stridedattention_pa_t_kernel(tc, q, k, x, wv, out):
     nc = tc.nc
     with ExitStack() as ctx:
         const = ctx.enter_context(tc.tile_pool(name="const", bufs=1))
-        loads = ctx.enter_context(tc.tile_pool(name="loads", bufs=B))
+        loads = ctx.enter_context(tc.tile_pool(name="loads", bufs=3))
         work = ctx.enter_context(tc.tile_pool(name="work", bufs=2))
         psum = ctx.enter_context(tc.psum_pool(name="psum", bufs=1))
+        ctx.enter_context(tc.manual_schedule())
 
-        wv_rows = const.tile([P, TILES * D], BF16)
-        nc.sync.dma_start(
-            out=wv_rows[:].rearrange("p (a c) -> p a c", a=TILES),
-            in_=wv.rearrange("(a p) c -> p a c", p=P),
-        )
-        x_of, q_of, k_of = [], [], []
-        for b in range(B):
-            x_rows = loads.tile([P, TILES * D], BF16)
-            nc.sync.dma_start(
-                out=x_rows[:].rearrange("p (u c) -> p u c", u=2),
-                in_=x[b].rearrange("(u p e) c -> p u (e c)", u=2, e=2),
-            )
+        x_of, q_of, k_of = {}, {}, {}
+
+        def load_sequence(b):
             q_rows = loads.tile([P, H * TILES * HD], BF16)
             nc.sync.dma_start(
                 out=q_rows[:].rearrange("p (g d) -> p g d", d=HD),
@@ -54,9 +48,20 @@ def tile_stridedattention_pa_t_kernel(tc, q, k, x, wv, out):
                 out=k_rows[:].rearrange("p (g d) -> p g d", d=HD),
                 in_=k[b].rearrange("h (i p) d -> p (h i) d", p=P),
             )
-            x_of.append(x_rows)
-            q_of.append(q_rows)
-            k_of.append(k_rows)
+            x_rows = loads.tile([P, TILES * D], BF16)
+            nc.sync.dma_start(
+                out=x_rows[:].rearrange("p (u c) -> p u c", u=2),
+                in_=x[b].rearrange("(u p e) c -> p u (e c)", u=2, e=2),
+            )
+            q_of[b], k_of[b], x_of[b] = q_rows, k_rows, x_rows
+
+        load_sequence(0)
+        wv_rows = const.tile([P, TILES * D], BF16)
+        nc.sync.dma_start(
+            out=wv_rows[:].rearrange("p (a c) -> p a c", a=TILES),
+            in_=wv.rearrange("(a p) c -> p a c", p=P),
+        )
+        load_sequence(1)
 
         ident_bf = const.tile([P, P], BF16)
         make_identity(nc, ident_bf[:])
@@ -71,32 +76,32 @@ def tile_stridedattention_pa_t_kernel(tc, q, k, x, wv, out):
             nc.vector.memset(e_rows[:], 0.0)
             e_buffers.append(e_rows)
 
-        def flip(rows, copy_out):
+        def flip(rows, what):
             words = rows[:].bitcast(F32)
-            grouped = work.tile([P, TILES * P * PACK], BF16, align_bytes=64, tag="grouped", bufs=3)
+            grouped = work.tile([P, TILES * P * PACK], BF16, align_bytes=64, tag=what + "_grouped")
             grouped_words = grouped[:].bitcast(F32).rearrange("p (a r u) -> p a r u", a=TILES, u=2)
             for half in range(2):
-                flipped = psum.tile([P, 2, 2, P], F32, tag="flipped", bufs=3)
+                flipped = psum.tile([P, 2, 2, P], F32, tag="flipped", bufs=2)
                 for a in range(2):
                     for u in range(2):
                         first = ((2 * half + a) * 2 + u) * P
                         nc.tensor.transpose(flipped[:, a, u, :], words[:, first : first + P], ident_f32[:])
-                copy_out(
+                nc.scalar.copy(
                     out=grouped_words[:, 2 * half : 2 * half + 2, :, :],
                     in_=flipped[:].rearrange("p a u r -> p a r u"),
                 )
             return grouped
 
-        def quantise(grouped, what, bufs):
+        def quantise(grouped, what):
             width = grouped.shape[1] // PACK
-            codes = work.tile([P, width], U32, align_bytes=64, tag=what + "_codes", bufs=bufs)
-            scales = work.tile([P, width], U8, align_bytes=64, tag=what + "_scales", bufs=bufs)
+            codes = work.tile([P, width], U32, align_bytes=64, tag=what + "_codes")
+            scales = work.tile([P, width], U8, align_bytes=64, tag=what + "_scales")
             nc.vector.quantize_mx(out=codes[:].bitcast(FP8X4), scales=scales[:], in_=grouped[:])
             return codes, scales
 
         def project_values(step, x_mx, w_mx):
             h = step % H
-            v_ps = psum.tile([P, PACK, HD], F32, tag="v_ps", bufs=1)
+            v_ps = psum.tile([P, PACK, HD], F32, tag="v_ps")
             for a in range(PACK):
                 nc.tensor.matmul_mx(
                     out=v_ps[:, a, :],
@@ -107,7 +112,10 @@ def tile_stridedattention_pa_t_kernel(tc, q, k, x, wv, out):
                     start=True,
                     stop=True,
                 )
-            v_grouped = work.tile([P, HD * PACK], BF16, align_bytes=64, tag="v_grouped", bufs=3)
+            return v_ps
+
+        def regroup_values(v_ps):
+            v_grouped = work.tile([P, HD * PACK], BF16, align_bytes=64, tag="v_grouped")
             nc.scalar.copy(
                 out=v_grouped[:].rearrange("p (f a) -> p f a", a=PACK),
                 in_=v_ps[:].rearrange("p a f -> p f a"),
@@ -116,43 +124,50 @@ def tile_stridedattention_pa_t_kernel(tc, q, k, x, wv, out):
 
         def flip_q_and_k(step):
             b, h = divmod(step, H)
-            qk_ps = psum.tile([P, 2 * T], BF16, tag="qk_ps", bufs=1)
+            qk_ps = psum.tile([P, 2 * T], BF16, tag="qk_ps")
             for i in range(TILES):
                 rows = slice((h * TILES + i) * HD, (h * TILES + i + 1) * HD)
                 nc.tensor.transpose(qk_ps[:, i * P : (i + 1) * P], q_of[b][:, rows], ident_bf[:])
                 nc.tensor.transpose(qk_ps[:, T + i * P : T + (i + 1) * P], k_of[b][:, rows], ident_bf[:])
-            qk_t = work.tile([P, 2 * T], BF16, tag="qk_t", bufs=2)
-            nc.scalar.copy(out=qk_t[:], in_=qk_ps[:])
+            qk_t = work.tile([P, 2 * T], BF16, tag="qk_t")
+            nc.vector.tensor_copy(out=qk_t[:], in_=qk_ps[:])
             return qk_t
 
-        def softmax_numerators(step, qk_t):
-            e_rows = e_buffers[step % 2]
-            neg_max = work.tile([P, TILES], F32, tag="neg_max", bufs=2)
-            row_sum = work.tile([P, TILES], F32, tag="row_sum", bufs=5)
+        def scores(qk_t):
+            s_02 = psum.tile([P, T], F32, tag="s_02")
+            s_1 = psum.tile([P, T], F32, tag="s_1")
+            s_3 = psum.tile([P, T], F32, tag="s_3")
+            s_ps = [s_02[:, : SEEN[0]], s_1[:, : SEEN[1]], s_02[:, SEEN[0] :], s_3[:, :]]
             for i in range(TILES):
-                seen = (i + 1) * P
-                s_ps = psum.tile([P, T], F32, tag="s_ps", bufs=2)
                 nc.tensor.matmul(
-                    s_ps[:, :seen], lhsT=qk_t[:, i * P : (i + 1) * P], rhs=qk_t[:, T : T + seen],
+                    s_ps[i], lhsT=qk_t[:, i * P : (i + 1) * P], rhs=qk_t[:, T : T + SEEN[i]],
                     start=True, stop=False,
                 )
                 nc.tensor.matmul(
-                    s_ps[:, seen - STRIDE : seen], lhsT=ident_bf[:], rhs=later_block[:],
+                    s_ps[i][:, SEEN[i] - STRIDE :], lhsT=ident_bf[:], rhs=later_block[:],
                     start=False, stop=True,
                 )
-                s_neg = work.tile([P, T], F32, tag="s_neg", bufs=4)
+            s_neg = work.tile([P, sum(SEEN)], F32, tag="s_neg")
+            neg_max = work.tile([P, TILES], F32, tag="neg_max")
+            for i in range(TILES):
                 nc.vector.tensor_scalar(
-                    out=s_neg[:, :seen], in0=s_ps[:, :seen], scalar1=-SCALE, scalar2=None,
+                    out=s_neg[:, FIRST[i] : FIRST[i] + SEEN[i]], in0=s_ps[i], scalar1=-SCALE, scalar2=None,
                     op0=MULT, op1=MIN, accum_out=neg_max[:, i : i + 1],
                 )
+            return s_neg, neg_max
+
+        def exponentials(step, s_neg, neg_max):
+            e_rows = e_buffers[step % 2]
+            row_sum = work.tile([P, TILES], F32, tag="row_sum", bufs=5)
+            for i in range(TILES):
                 nc.scalar.activation(
-                    out=e_rows[:, i * T : i * T + seen], in_=s_neg[:, :seen], func=EXP,
-                    bias=neg_max[:, i : i + 1], scale=-1.0, accum_out=row_sum[:, i : i + 1],
+                    out=e_rows[:, i * T : i * T + SEEN[i]], in_=s_neg[:, FIRST[i] : FIRST[i] + SEEN[i]],
+                    func=EXP, bias=neg_max[:, i : i + 1], scale=-1.0, accum_out=row_sum[:, i : i + 1],
                 )
             return e_rows, row_sum
 
         def attend(e_mx, v_mx):
-            o_ps = psum.tile([P, TILES, HD], F32, tag="o_ps", bufs=1)
+            o_ps = psum.tile([P, TILES, HD], F32, tag="o_ps")
             for i in range(TILES):
                 nc.tensor.matmul_mx(
                     out=o_ps[:, i, :],
@@ -167,7 +182,7 @@ def tile_stridedattention_pa_t_kernel(tc, q, k, x, wv, out):
 
         def normalise_and_store(step, o_ps, row_sum):
             b, h = divmod(step, H)
-            inv_sum = work.tile([P, TILES], F32, tag="inv_sum", bufs=2)
+            inv_sum = work.tile([P, TILES], F32, tag="inv_sum")
             nc.vector.reciprocal(out=inv_sum[:], in_=row_sum[:])
             o_sb = work.tile([P, TILES, HD], F32, tag="o_sb", bufs=3)
             nc.vector.tensor_tensor(
@@ -177,31 +192,39 @@ def tile_stridedattention_pa_t_kernel(tc, q, k, x, wv, out):
                 out=out[b].rearrange("(i p) c -> p i c", p=P)[:, :, h * HD : (h + 1) * HD], in_=o_sb[:]
             )
 
-        w_mx = quantise(flip(wv_rows, nc.vector.tensor_copy), "w", 1)
-        x_mx = {0: quantise(flip(x_of[0], nc.vector.tensor_copy), "x", 3)}
-        v_grouped, v_mx, qk_t, e_done, e_grouped, e_mx, o_done = {}, {}, {}, {}, {}, {}, {}
-        qk_t[0] = flip_q_and_k(0)
-        for step in range(H):
-            v_grouped[step] = project_values(step, x_mx[0], w_mx)
-            v_mx[step] = quantise(v_grouped[step], "v", 8)
-        x_mx[1] = quantise(flip(x_of[1], nc.vector.tensor_copy), "x", 3)
+        def is_step(s):
+            return 0 <= s < STEPS
 
-        for n in range(STEPS + 3):
-            if 1 <= n <= STEPS:
-                e_grouped[n - 1] = flip(e_done[n - 1][0], nc.scalar.copy)
-            if n >= 3:
-                normalise_and_store(n - 3, o_done[n - 3], e_done[n - 3][1])
-            if n < STEPS:
-                e_done[n] = softmax_numerators(n, qk_t[n])
-            if 1 <= n <= STEPS:
-                e_mx[n - 1] = quantise(e_grouped[n - 1], "e", 3)
-            if H <= n + 3 < STEPS:
-                v_mx[n + 3] = quantise(v_grouped[n + 3], "v", 8)
-            if n + 1 < STEPS:
-                qk_t[n + 1] = flip_q_and_k(n + 1)
-            if n % H == H - 1 and (n + 5) // H < B:
-                x_mx[(n + 5) // H] = quantise(flip(x_of[(n + 5) // H], nc.vector.tensor_copy), "x", 3)
-            if 2 <= n < STEPS + 2:
-                o_done[n - 2] = attend(e_mx[n - 2], v_mx[n - 2])
-            if n + 4 < STEPS:
-                v_grouped[n + 4] = project_values(n + 4, x_mx[(n + 4) // H], w_mx)
+        x_grouped, x_mx, w_mx = {}, {}, {}
+        qk_t, s_done, e_done, e_grouped, e_mx = {}, {}, {}, {}, {}
+        v_ps, v_grouped, v_mx, o_ps = {}, {}, {}, {}
+        for n in range(-2, STEPS + 3):
+            if is_step(n - 3):
+                normalise_and_store(n - 3, o_ps[n - 3], e_done[n - 3][1])
+            if is_step(n - 2):
+                e_mx[n - 2] = quantise(e_grouped[n - 2], "e")
+                v_mx[n - 2] = quantise(v_grouped[n - 2], "v")
+            if is_step(n + 1) and (n + 1) % H == 0:
+                if n + 1 == 0:
+                    w_mx[0] = quantise(x_grouped["wv"], "w")
+                x_mx[(n + 1) // H] = quantise(x_grouped[(n + 1) // H], "x")
+            if is_step(n) and n % H == 0 and n // H + 2 < B:
+                load_sequence(n // H + 2)
+            if is_step(n):
+                e_done[n] = exponentials(n, s_done[n][0], s_done[n][1])
+            if is_step(n - 1):
+                v_grouped[n - 1] = regroup_values(v_ps[n - 1])
+            if is_step(n + 2):
+                qk_t[n + 2] = flip_q_and_k(n + 2)
+            if is_step(n - 1):
+                e_grouped[n - 1] = flip(e_done[n - 1][0], "e")
+            if is_step(n + 1):
+                s_done[n + 1] = scores(qk_t[n + 1])
+            if is_step(n - 2):
+                o_ps[n - 2] = attend(e_mx[n - 2], v_mx[n - 2])
+            if is_step(n):
+                v_ps[n] = project_values(n, x_mx[n // H], w_mx[0])
+            if is_step(n + 2) and (n + 2) % H == 0:
+                if n + 2 == 0:
+                    x_grouped["wv"] = flip(wv_rows, "w")
+                x_grouped[(n + 2) // H] = flip(x_of[(n + 2) // H], "x")

@@ -20,6 +20,7 @@ TILES = T // P
 SCALE = HD**-0.5
 MASKED = -1.0e30
 STEPS = B * H
+AHEAD = 6
 SEEN = [(i + 1) * P for i in range(TILES)]
 FIRST = [sum(SEEN[:i]) for i in range(TILES)]
 
@@ -37,31 +38,38 @@ def tile_stridedattention_pa_t_kernel(tc, q, k, x, wv, out):
 
         x_of, q_of, k_of = {}, {}, {}
 
-        def load_sequence(b):
-            q_rows = loads.tile([P, H * TILES * HD], BF16)
+        def load_head(step):
+            b, h = divmod(step, H)
+            q_rows = loads.tile([P, TILES * HD], BF16, bufs=8)
             nc.sync.dma_start(
-                out=q_rows[:].rearrange("p (g d) -> p g d", d=HD),
-                in_=q[b].rearrange("h (i p) d -> p (h i) d", p=P),
+                out=q_rows[:].rearrange("p (i d) -> p i d", d=HD),
+                in_=q[b][h].rearrange("(i p) d -> p i d", p=P),
             )
-            k_rows = loads.tile([P, H * TILES * HD], BF16)
+            k_rows = loads.tile([P, TILES * HD], BF16, bufs=8)
             nc.sync.dma_start(
-                out=k_rows[:].rearrange("p (g d) -> p g d", d=HD),
-                in_=k[b].rearrange("h (i p) d -> p (h i) d", p=P),
+                out=k_rows[:].rearrange("p (i d) -> p i d", d=HD),
+                in_=k[b][h].rearrange("(i p) d -> p i d", p=P),
             )
+            q_of[step], k_of[step] = q_rows, k_rows
+
+        def load_x(b):
             x_rows = loads.tile([P, TILES * D], BF16)
             nc.sync.dma_start(
                 out=x_rows[:].rearrange("p (u c) -> p u c", u=2),
                 in_=x[b].rearrange("(u p e) c -> p u (e c)", u=2, e=2),
             )
-            q_of[b], k_of[b], x_of[b] = q_rows, k_rows, x_rows
+            x_of[b] = x_rows
 
-        load_sequence(0)
+        load_head(0)
+        load_head(1)
         wv_rows = const.tile([P, TILES * D], BF16)
         nc.sync.dma_start(
             out=wv_rows[:].rearrange("p (a c) -> p a c", a=TILES),
             in_=wv.rearrange("(a p) c -> p a c", p=P),
         )
-        load_sequence(1)
+        load_x(0)
+        load_head(2)
+        load_head(3)
 
         ident_bf = const.tile([P, P], BF16)
         make_identity(nc, ident_bf[:])
@@ -123,12 +131,11 @@ def tile_stridedattention_pa_t_kernel(tc, q, k, x, wv, out):
             return v_grouped
 
         def flip_q_and_k(step):
-            b, h = divmod(step, H)
             qk_ps = psum.tile([P, 2 * T], BF16, tag="qk_ps")
             for i in range(TILES):
-                rows = slice((h * TILES + i) * HD, (h * TILES + i + 1) * HD)
-                nc.tensor.transpose(qk_ps[:, i * P : (i + 1) * P], q_of[b][:, rows], ident_bf[:])
-                nc.tensor.transpose(qk_ps[:, T + i * P : T + (i + 1) * P], k_of[b][:, rows], ident_bf[:])
+                rows = slice(i * HD, (i + 1) * HD)
+                nc.tensor.transpose(qk_ps[:, i * P : (i + 1) * P], q_of[step][:, rows], ident_bf[:])
+                nc.tensor.transpose(qk_ps[:, T + i * P : T + (i + 1) * P], k_of[step][:, rows], ident_bf[:])
             qk_t = work.tile([P, 2 * T], BF16, tag="qk_t")
             nc.vector.tensor_copy(out=qk_t[:], in_=qk_ps[:])
             return qk_t
@@ -158,7 +165,7 @@ def tile_stridedattention_pa_t_kernel(tc, q, k, x, wv, out):
 
         def exponentials(step, s_neg, neg_max):
             e_rows = e_buffers[step % 2]
-            row_sum = work.tile([P, TILES], F32, tag="row_sum", bufs=5)
+            row_sum = work.tile([P, TILES], F32, tag="row_sum", bufs=4)
             for i in range(TILES):
                 nc.scalar.activation(
                     out=e_rows[:, i * T : i * T + SEEN[i]], in_=s_neg[:, FIRST[i] : FIRST[i] + SEEN[i]],
@@ -180,10 +187,13 @@ def tile_stridedattention_pa_t_kernel(tc, q, k, x, wv, out):
                 )
             return o_ps
 
-        def normalise_and_store(step, o_ps, row_sum):
-            b, h = divmod(step, H)
-            inv_sum = work.tile([P, TILES], F32, tag="inv_sum")
+        def invert(row_sum):
+            inv_sum = work.tile([P, TILES], F32, tag="inv_sum", bufs=3)
             nc.vector.reciprocal(out=inv_sum[:], in_=row_sum[:])
+            return inv_sum
+
+        def normalise_and_store(step, o_ps, inv_sum):
+            b, h = divmod(step, H)
             o_sb = work.tile([P, TILES, HD], F32, tag="o_sb", bufs=3)
             nc.vector.tensor_tensor(
                 out=o_sb[:], in0=o_ps[:], in1=inv_sum[:].unsqueeze(2).to_broadcast([P, TILES, HD]), op=MULT
@@ -196,35 +206,35 @@ def tile_stridedattention_pa_t_kernel(tc, q, k, x, wv, out):
             return 0 <= s < STEPS
 
         x_grouped, x_mx, w_mx = {}, {}, {}
-        qk_t, s_done, e_done, e_grouped, e_mx = {}, {}, {}, {}, {}
-        v_ps, v_grouped, v_mx, o_ps = {}, {}, {}, {}
+        qk_t, s_done, e_done, e_grouped, e_mx, inv_sum = {}, {}, {}, {}, {}, {}
+        v_grouped, v_mx, o_ps = {}, {}, {}
         for n in range(-2, STEPS + 3):
             if is_step(n - 3):
-                normalise_and_store(n - 3, o_ps[n - 3], e_done[n - 3][1])
+                normalise_and_store(n - 3, o_ps[n - 3], inv_sum[n - 3])
             if is_step(n - 2):
                 e_mx[n - 2] = quantise(e_grouped[n - 2], "e")
                 v_mx[n - 2] = quantise(v_grouped[n - 2], "v")
-            if is_step(n + 1) and (n + 1) % H == 0:
-                if n + 1 == 0:
+                inv_sum[n - 2] = invert(e_done[n - 2][1])
+            if is_step(n - 1) and (n - 1) % H == 0:
+                if n - 1 == 0:
                     w_mx[0] = quantise(x_grouped["wv"], "w")
-                x_mx[(n + 1) // H] = quantise(x_grouped[(n + 1) // H], "x")
-            if is_step(n) and n % H == 0 and n // H + 2 < B:
-                load_sequence(n // H + 2)
+                x_mx[(n - 1) // H] = quantise(x_grouped[(n - 1) // H], "x")
+            if H <= n + AHEAD < STEPS:
+                load_head(n + AHEAD)
+                if (n + AHEAD) % H == 0:
+                    load_x((n + AHEAD) // H)
             if is_step(n):
                 e_done[n] = exponentials(n, s_done[n][0], s_done[n][1])
-            if is_step(n - 1):
-                v_grouped[n - 1] = regroup_values(v_ps[n - 1])
             if is_step(n + 2):
                 qk_t[n + 2] = flip_q_and_k(n + 2)
-            if is_step(n - 1):
-                e_grouped[n - 1] = flip(e_done[n - 1][0], "e")
             if is_step(n + 1):
                 s_done[n + 1] = scores(qk_t[n + 1])
+            if is_step(n - 1):
+                e_grouped[n - 1] = flip(e_done[n - 1][0], "e")
+                v_grouped[n - 1] = regroup_values(project_values(n - 1, x_mx[(n - 1) // H], w_mx[0]))
             if is_step(n - 2):
                 o_ps[n - 2] = attend(e_mx[n - 2], v_mx[n - 2])
-            if is_step(n):
-                v_ps[n] = project_values(n, x_mx[n // H], w_mx[0])
-            if is_step(n + 2) and (n + 2) % H == 0:
-                if n + 2 == 0:
+            if is_step(n) and n % H == 0:
+                if n == 0:
                     x_grouped["wv"] = flip(wv_rows, "w")
-                x_grouped[(n + 2) // H] = flip(x_of[(n + 2) // H], "x")
+                x_grouped[n // H] = flip(x_of[n // H], "x")

@@ -5,12 +5,15 @@ from concourse.masks import make_identity
 
 BF16 = mybir.dt.bfloat16
 F32 = mybir.dt.float32
+I32 = mybir.dt.int32
 U32 = mybir.dt.uint32
 U8 = mybir.dt.uint8
 FP8X4 = mybir.dt.float8_e4m3fn_x4
 EXP = mybir.ActivationFunctionType.Exp
 MULT = mybir.AluOpType.mult
-MIN = mybir.AluOpType.min
+ADD = mybir.AluOpType.add
+MAX = mybir.AluOpType.max
+AXIS_X = mybir.AxisListType.X
 
 B, T, D, H, HD = 8, 512, 512, 4, 128
 STRIDE = 64
@@ -19,10 +22,12 @@ PACK = 4
 TILES = T // P
 SCALE = HD**-0.5
 MASKED = -1.0e30
-STEPS = B * H
-AHEAD = 6
+PAIRS = B * H // 2
 SEEN = [(i + 1) * P for i in range(TILES)]
-FIRST = [sum(SEEN[:i]) for i in range(TILES)]
+BANKS = [[(0, 3)], [(1, 3)], [(0, 2), (0, 0)], [(1, 2), (1, 0)], [(0, 1), (1, 1)]]
+GROUPS = [[(0, 3)], [(1, 3)], [(0, 2)], [(1, 2)], [(0, 1), (1, 1)], [(0, 0), (1, 0)]]
+GROUP_OF = {tile: g for g in range(len(GROUPS)) for tile in GROUPS[g]}
+AHEAD = 3
 
 FLOPS = 2 * B * T * D * D + 2 * 2 * B * H * T * T * HD
 
@@ -31,45 +36,53 @@ def tile_stridedattention_pa_t_kernel(tc, q, k, x, wv, out):
     nc = tc.nc
     with ExitStack() as ctx:
         const = ctx.enter_context(tc.tile_pool(name="const", bufs=1))
-        loads = ctx.enter_context(tc.tile_pool(name="loads", bufs=3))
+        loads = ctx.enter_context(tc.tile_pool(name="loads", bufs=8))
         work = ctx.enter_context(tc.tile_pool(name="work", bufs=2))
         psum = ctx.enter_context(tc.psum_pool(name="psum", bufs=1))
         ctx.enter_context(tc.manual_schedule())
 
-        x_of, q_of, k_of = {}, {}, {}
+        def place(n, m):
+            return 2 * (n // H) + m, n % H
 
-        def load_head(step):
-            b, h = divmod(step, H)
-            q_rows = loads.tile([P, TILES * HD], BF16, bufs=8)
+        q_of, k_of, x_of = {}, {}, {}
+
+        def load_member(n, m):
+            b, h = place(n, m)
+            q_rows = loads.tile([P, TILES * HD], BF16)
             nc.sync.dma_start(
                 out=q_rows[:].rearrange("p (i d) -> p i d", d=HD),
                 in_=q[b][h].rearrange("(i p) d -> p i d", p=P),
             )
-            k_rows = loads.tile([P, TILES * HD], BF16, bufs=8)
+            k_rows = loads.tile([P, TILES * HD], BF16)
             nc.sync.dma_start(
                 out=k_rows[:].rearrange("p (i d) -> p i d", d=HD),
                 in_=k[b][h].rearrange("(i p) d -> p i d", p=P),
             )
-            q_of[step], k_of[step] = q_rows, k_rows
+            q_of[n, m], k_of[n, m] = q_rows, k_rows
 
-        def load_x(b):
-            x_rows = loads.tile([P, TILES * D], BF16)
-            nc.sync.dma_start(
-                out=x_rows[:].rearrange("p (u c) -> p u c", u=2),
-                in_=x[b].rearrange("(u p e) c -> p u (e c)", u=2, e=2),
-            )
-            x_of[b] = x_rows
+        def load_x(bp):
+            x_0 = loads.tile([P, TILES * D], BF16, bufs=2)
+            nc.sync.dma_start(out=x_0[:], in_=x[2 * bp].rearrange("(p a) c -> p (a c)", a=PACK))
+            x_1 = loads.tile([P, TILES * D], BF16, bufs=2)
+            for quarter in range(TILES):
+                block = TILES - 1 - quarter
+                nc.sync.dma_start(
+                    out=x_1[32 * quarter : 32 * (quarter + 1), :],
+                    in_=x[2 * bp + 1][block * P : (block + 1) * P, :].rearrange("(p a) c -> p (a c)", a=PACK),
+                )
+            x_of[bp, 0], x_of[bp, 1] = x_0, x_1
 
-        load_head(0)
-        load_head(1)
+        load_member(0, 0)
+        load_member(0, 1)
         wv_rows = const.tile([P, TILES * D], BF16)
         nc.sync.dma_start(
             out=wv_rows[:].rearrange("p (a c) -> p a c", a=TILES),
             in_=wv.rearrange("(a p) c -> p a c", p=P),
         )
         load_x(0)
-        load_head(2)
-        load_head(3)
+        for n in range(1, AHEAD):
+            for m in range(2):
+                load_member(n, m)
 
         ident_bf = const.tile([P, P], BF16)
         make_identity(nc, ident_bf[:])
@@ -78,27 +91,34 @@ def tile_stridedattention_pa_t_kernel(tc, q, k, x, wv, out):
         later_block = const.tile([P, STRIDE], BF16)
         nc.vector.memset(later_block[0:STRIDE, :], MASKED)
         nc.vector.memset(later_block[STRIDE:P, :], 0.0)
-        e_buffers = []
+        e_buffers, r_buffers = [], []
         for j in range(2):
-            e_rows = const.tile([P, TILES * T], BF16, name="e_rows%d" % j)
-            nc.vector.memset(e_rows[:], 0.0)
+            e_rows = const.tile([P, len(GROUPS), 2, 2 * P], BF16, name="e_rows%d" % j)
+            nc.vector.memset(e_rows[:, 2, :, 192:256], 0.0)
+            nc.vector.memset(e_rows[:, 3, :, 0:64], 0.0)
+            nc.vector.memset(e_rows[:, 5, :, 64:192], 0.0)
             e_buffers.append(e_rows)
+            halves = const.tile([P, 2 * HD], U32, align_bytes=64, name="halves%d" % j)
+            nc.vector.memset(halves[:].bitcast(I32), 0)
+            r_buffers.append(halves)
 
-        def flip(rows, what):
-            words = rows[:].bitcast(F32)
-            grouped = work.tile([P, TILES * P * PACK], BF16, align_bytes=64, tag=what + "_grouped")
-            grouped_words = grouped[:].bitcast(F32).rearrange("p (a r u) -> p a r u", a=TILES, u=2)
-            for half in range(2):
-                flipped = psum.tile([P, 2, 2, P], F32, tag="flipped", bufs=2)
-                for a in range(2):
-                    for u in range(2):
-                        first = ((2 * half + a) * 2 + u) * P
-                        nc.tensor.transpose(flipped[:, a, u, :], words[:, first : first + P], ident_f32[:])
-                nc.scalar.copy(
-                    out=grouped_words[:, 2 * half : 2 * half + 2, :, :],
-                    in_=flipped[:].rearrange("p a u r -> p a r u"),
-                )
-            return grouped
+        def passing(shape, dtype):
+            bank = psum.tile(shape, dtype, tag="passing", bufs=5)
+            return bank
+
+        def flip_words(words):
+            flipped = passing([P, 2, 2, P], F32)
+            for a in range(2):
+                for u in range(2):
+                    nc.tensor.transpose(flipped[:, a, u, :], words[2 * a + u], ident_f32[:])
+            return flipped
+
+        def regroup(flipped, grouped, half):
+            out_words = grouped[:].bitcast(F32).rearrange("p (a r u) -> p a r u", r=P, u=2)
+            nc.scalar.copy(
+                out=out_words[:, 2 * half : 2 * half + 2, :, :],
+                in_=flipped[:].rearrange("p a u r -> p a r u"),
+            )
 
         def quantise(grouped, what):
             width = grouped.shape[1] // PACK
@@ -107,134 +127,314 @@ def tile_stridedattention_pa_t_kernel(tc, q, k, x, wv, out):
             nc.vector.quantize_mx(out=codes[:].bitcast(FP8X4), scales=scales[:], in_=grouped[:])
             return codes, scales
 
-        def project_values(step, x_mx, w_mx):
-            h = step % H
-            v_ps = psum.tile([P, PACK, HD], F32, tag="v_ps")
-            for a in range(PACK):
-                nc.tensor.matmul_mx(
-                    out=v_ps[:, a, :],
-                    lhsT=x_mx[0][:, a * P : (a + 1) * P].bitcast(FP8X4),
-                    lhsT_scale=x_mx[1][:, a * P : (a + 1) * P],
-                    rhs=w_mx[0][:, h * HD : (h + 1) * HD].bitcast(FP8X4),
-                    rhs_scale=w_mx[1][:, h * HD : (h + 1) * HD],
-                    start=True,
-                    stop=True,
-                )
-            return v_ps
+        def feature_words(rows, half):
+            words = rows[:].bitcast(F32)
+            return [words[:, (4 * half + j) * P : (4 * half + j + 1) * P] for j in range(4)]
 
-        def regroup_values(v_ps):
-            v_grouped = work.tile([P, HD * PACK], BF16, align_bytes=64, tag="v_grouped")
-            nc.scalar.copy(
-                out=v_grouped[:].rearrange("p (f a) -> p f a", a=PACK),
-                in_=v_ps[:].rearrange("p a f -> p f a"),
-            )
-            return v_grouped
+        qk_t, s_of, bias_of, sums_of = {}, {}, {}, {}
+        e_flipped, e_grouped, e_mx = {}, {}, {}
+        x_flipped, x_grouped, x_mx = {}, {}, {}
+        v_ps, v_grouped, v_mx, halves_of = {}, {}, {}, {}
+        o_ps, inv_of, o_of = {}, {}, {}
+        qk_ps = {}
 
-        def flip_q_and_k(step):
-            qk_ps = psum.tile([P, 2 * T], BF16, tag="qk_ps")
+        def flip_q_and_k(n, m):
+            both = passing([P, 2 * T], BF16)
             for i in range(TILES):
                 rows = slice(i * HD, (i + 1) * HD)
-                nc.tensor.transpose(qk_ps[:, i * P : (i + 1) * P], q_of[step][:, rows], ident_bf[:])
-                nc.tensor.transpose(qk_ps[:, T + i * P : T + (i + 1) * P], k_of[step][:, rows], ident_bf[:])
-            qk_t = work.tile([P, 2 * T], BF16, tag="qk_t")
-            nc.vector.tensor_copy(out=qk_t[:], in_=qk_ps[:])
-            return qk_t
+                key_block = i if m == 0 else TILES - 1 - i
+                nc.tensor.transpose(both[:, i * P : (i + 1) * P], q_of[n, m][:, rows], ident_bf[:])
+                nc.tensor.transpose(
+                    both[:, T + key_block * P : T + (key_block + 1) * P], k_of[n, m][:, rows], ident_bf[:]
+                )
+            qk_ps[n, m] = both
 
-        def scores(qk_t):
-            s_02 = psum.tile([P, T], F32, tag="s_02")
-            s_1 = psum.tile([P, T], F32, tag="s_1")
-            s_3 = psum.tile([P, T], F32, tag="s_3")
-            s_ps = [s_02[:, : SEEN[0]], s_1[:, : SEEN[1]], s_02[:, SEEN[0] :], s_3[:, :]]
-            for i in range(TILES):
+        def copy_q_and_k(n, m):
+            copied = work.tile([P, 2 * T], BF16, tag="qk_t%d" % m)
+            nc.vector.tensor_copy(out=copied[:], in_=qk_ps[n, m][:])
+            qk_t[n, m] = copied
+
+        def scores(n, bank):
+            s_ps = psum.tile([P, T], F32, tag="scores", bufs=3)
+            first = 0
+            for m, i in BANKS[bank]:
+                s_tile = s_ps[:, first : first + SEEN[i]]
+                keys = T if m == 0 else 2 * T - SEEN[i]
                 nc.tensor.matmul(
-                    s_ps[i], lhsT=qk_t[:, i * P : (i + 1) * P], rhs=qk_t[:, T : T + SEEN[i]],
+                    s_tile, lhsT=qk_t[n, m][:, i * P : (i + 1) * P], rhs=qk_t[n, m][:, keys : keys + SEEN[i]],
                     start=True, stop=False,
                 )
+                later = SEEN[i] - STRIDE if m == 0 else STRIDE
                 nc.tensor.matmul(
-                    s_ps[i][:, SEEN[i] - STRIDE :], lhsT=ident_bf[:], rhs=later_block[:],
+                    s_tile[:, later : later + STRIDE], lhsT=ident_bf[:], rhs=later_block[:],
                     start=False, stop=True,
                 )
-            s_neg = work.tile([P, sum(SEEN)], F32, tag="s_neg")
-            neg_max = work.tile([P, TILES], F32, tag="neg_max")
-            for i in range(TILES):
-                nc.vector.tensor_scalar(
-                    out=s_neg[:, FIRST[i] : FIRST[i] + SEEN[i]], in0=s_ps[i], scalar1=-SCALE, scalar2=None,
-                    op0=MULT, op1=MIN, accum_out=neg_max[:, i : i + 1],
-                )
-            return s_neg, neg_max
+                first += SEEN[i]
+            s_of[n, bank] = s_ps
 
-        def exponentials(step, s_neg, neg_max):
-            e_rows = e_buffers[step % 2]
-            row_sum = work.tile([P, TILES], F32, tag="row_sum", bufs=4)
-            for i in range(TILES):
+        def maxima(n, bank):
+            tiles = BANKS[bank]
+            s_ps = s_of[n, bank]
+            row_max = work.tile([P, 2], F32, tag="row_max", bufs=4)
+            if bank == 4:
+                nc.vector.tensor_reduce(
+                    out=row_max[:], in_=s_ps[:].rearrange("p (j c) -> p j c", j=2), axis=AXIS_X, op=MAX
+                )
+            else:
+                first = 0
+                for j in range(len(tiles)):
+                    seen = SEEN[tiles[j][1]]
+                    nc.vector.tensor_reduce(
+                        out=row_max[:, j : j + 1], in_=s_ps[:, first : first + seen], axis=AXIS_X, op=MAX
+                    )
+                    first += seen
+            bias = work.tile([P, 2], F32, tag="bias", bufs=4)
+            used = len(tiles)
+            nc.gpsimd.tensor_scalar(
+                out=bias[:, :used], in0=row_max[:, :used], scalar1=-SCALE, scalar2=0.0, op0=MULT, op1=ADD
+            )
+            bias_of[n, bank] = bias
+
+        def exponentials(n, bank):
+            s_ps, bias = s_of[n, bank], bias_of[n, bank]
+            if bank == 0:
+                row_sum = work.tile([P, 2 * TILES], F32, tag="row_sum", bufs=3)
+                sums_of[n] = row_sum
+            first = 0
+            for j in range(len(BANKS[bank])):
+                m, i = BANKS[bank][j]
+                seen = SEEN[i]
+                start = 0 if m == 0 else (T - seen) // 2
+                target = e_buffers[n % 2][:, GROUP_OF[m, i], :, start : start + seen // 2]
                 nc.scalar.activation(
-                    out=e_rows[:, i * T : i * T + SEEN[i]], in_=s_neg[:, FIRST[i] : FIRST[i] + SEEN[i]],
-                    func=EXP, bias=neg_max[:, i : i + 1], scale=-1.0, accum_out=row_sum[:, i : i + 1],
+                    out=target.rearrange("p u (w e) -> p u w e", e=2),
+                    in_=s_ps[:, first : first + seen].rearrange("p (w u e) -> p u w e", u=2, e=2),
+                    func=EXP, bias=bias[:, j : j + 1], scale=SCALE,
+                    accum_out=sums_of[n][:, 2 * i + m : 2 * i + m + 1],
                 )
-            return e_rows, row_sum
+                first += seen
 
-        def attend(e_mx, v_mx):
-            o_ps = psum.tile([P, TILES, HD], F32, tag="o_ps")
-            for i in range(TILES):
+        def flip_e(n, f):
+            words = e_buffers[n % 2][:].rearrange("p g u c -> p (g u c)").bitcast(F32)
+            e_flipped[n, f] = flip_words([words[:, (4 * f + j) * P : (4 * f + j + 1) * P] for j in range(4)])
+
+        def copy_e(n, f):
+            grouped = work.tile([P, 2 * P * PACK], BF16, align_bytes=64, tag="e_grouped", bufs=3)
+            regroup(e_flipped[n, f], grouped, 0)
+            e_grouped[n, f] = grouped
+
+        def quantise_e(n, f):
+            e_mx[n, f] = quantise(e_grouped[n, f], "e%d" % f)
+
+        def flip_x(key, rows, half):
+            x_flipped[key, half] = flip_words(feature_words(rows, half))
+
+        def copy_x(key, half):
+            if half == 0:
+                grouped = work.tile([P, TILES * P * PACK], BF16, align_bytes=64, tag="x_grouped")
+                x_grouped[key] = grouped
+            regroup(x_flipped[key, half], x_grouped[key], half)
+
+        def quantise_x(key):
+            x_mx[key] = quantise(x_grouped[key], "w" if key == "wv" else "x%d" % key[1])
+
+        def project_values(n, m):
+            bp, h = n // H, n % H
+            codes, scales = x_mx[bp, m]
+            w_codes, w_scales = x_mx["wv"]
+            bank = passing([P, PACK, HD], F32)
+            for a in range(PACK):
                 nc.tensor.matmul_mx(
-                    out=o_ps[:, i, :],
-                    lhsT=e_mx[0][:, i * P : (i + 1) * P].bitcast(FP8X4),
-                    lhsT_scale=e_mx[1][:, i * P : (i + 1) * P],
-                    rhs=v_mx[0][:].bitcast(FP8X4),
-                    rhs_scale=v_mx[1][:],
+                    out=bank[:, a, :],
+                    lhsT=codes[:, a * P : (a + 1) * P].bitcast(FP8X4),
+                    lhsT_scale=scales[:, a * P : (a + 1) * P],
+                    rhs=w_codes[:, h * HD : (h + 1) * HD].bitcast(FP8X4),
+                    rhs_scale=w_scales[:, h * HD : (h + 1) * HD],
                     start=True,
                     stop=True,
                 )
-            return o_ps
+            v_ps[n, m] = bank
 
-        def invert(row_sum):
-            inv_sum = work.tile([P, TILES], F32, tag="inv_sum", bufs=3)
-            nc.vector.reciprocal(out=inv_sum[:], in_=row_sum[:])
-            return inv_sum
+        def copy_v(n, m):
+            if m == 0:
+                grouped = work.tile([P, 2 * HD * PACK], BF16, align_bytes=64, tag="v_grouped")
+                v_grouped[n] = grouped
+            nc.scalar.copy(
+                out=v_grouped[n][:, m * HD * PACK : (m + 1) * HD * PACK].rearrange("p (f a) -> p f a", a=PACK),
+                in_=v_ps[n, m][:].rearrange("p a f -> p f a"),
+            )
 
-        def normalise_and_store(step, o_ps, inv_sum):
-            b, h = divmod(step, H)
-            o_sb = work.tile([P, TILES, HD], F32, tag="o_sb", bufs=3)
+        def quantise_v(n):
+            v_mx[n] = quantise(v_grouped[n], "v")
+
+        def copy_halves(n, m):
+            rows = slice(m * P // 2, (m + 1) * P // 2)
+            cols = slice(m * HD, (m + 1) * HD)
+            nc.vector.tensor_copy(
+                out=r_buffers[n % 2][rows, cols].bitcast(I32), in_=v_mx[n][0][rows, cols].bitcast(I32)
+            )
+
+        def attend(n, group, bank, first, width, codes, member):
+            e_codes, e_scales = e_mx[n, group // 2]
+            cols = slice((group % 2) * P, (group % 2 + 1) * P)
+            nc.tensor.matmul_mx(
+                out=bank[:, first : first + width],
+                lhsT=e_codes[:, cols].bitcast(FP8X4),
+                lhsT_scale=e_scales[:, cols],
+                rhs=codes[:, member * HD : member * HD + width].bitcast(FP8X4),
+                rhs_scale=v_mx[n][1][:, member * HD : member * HD + width],
+                start=True,
+                stop=True,
+            )
+
+        def attend_high(n):
+            bank = passing([P, 4 * HD], F32)
+            for j in range(4):
+                group = (2 + j) % 4
+                attend(n, group, bank, j * HD, HD, v_mx[n][0], j % 2)
+            o_ps[n, 1] = bank
+
+        def attend_low(n):
+            bank = passing([P, 4 * HD], F32)
+            for j in range(2):
+                attend(n, 5 - j, bank, 2 * j * HD, 2 * HD, r_buffers[n % 2], 0)
+            o_ps[n, 0] = bank
+
+        def invert(n):
+            inv = work.tile([P, 2 * TILES], F32, tag="inv_sum")
+            nc.vector.reciprocal(out=inv[:], in_=sums_of[n][:])
+            inv_of[n] = inv
+
+        def normalise(n, high):
+            if high:
+                o_sb = work.tile([P, 2 * TILES, HD], F32, tag="o_sb", bufs=3)
+                o_of[n] = o_sb
+            slots = slice(4 * high, 4 * high + 4)
             nc.vector.tensor_tensor(
-                out=o_sb[:], in0=o_ps[:], in1=inv_sum[:].unsqueeze(2).to_broadcast([P, TILES, HD]), op=MULT
-            )
-            nc.sync.dma_start(
-                out=out[b].rearrange("(i p) c -> p i c", p=P)[:, :, h * HD : (h + 1) * HD], in_=o_sb[:]
+                out=o_of[n][:, slots, :],
+                in0=o_ps[n, high][:].rearrange("p (s f) -> p s f", f=HD),
+                in1=inv_of[n][:, slots].unsqueeze(2).to_broadcast([P, 4, HD]),
+                op=MULT,
             )
 
-        def is_step(s):
-            return 0 <= s < STEPS
+        def store(n, high):
+            for m in range(2):
+                b, h = place(n, m)
+                nc.sync.dma_start(
+                    out=out[b].rearrange("(i p) c -> p i c", p=P)[:, 2 * high : 2 * high + 2, h * HD : (h + 1) * HD],
+                    in_=o_of[n][:].rearrange("p (i m) f -> p i m f", m=2)[:, 2 * high : 2 * high + 2, m, :],
+                )
 
-        x_grouped, x_mx, w_mx = {}, {}, {}
-        qk_t, s_done, e_done, e_grouped, e_mx, inv_sum = {}, {}, {}, {}, {}, {}
-        v_grouped, v_mx, o_ps = {}, {}, {}
-        for n in range(-2, STEPS + 3):
-            if is_step(n - 3):
-                normalise_and_store(n - 3, o_ps[n - 3], inv_sum[n - 3])
-            if is_step(n - 2):
-                e_mx[n - 2] = quantise(e_grouped[n - 2], "e")
-                v_mx[n - 2] = quantise(v_grouped[n - 2], "v")
-                inv_sum[n - 2] = invert(e_done[n - 2][1])
-            if is_step(n - 1) and (n - 1) % H == 0:
-                if n - 1 == 0:
-                    w_mx[0] = quantise(x_grouped["wv"], "w")
-                x_mx[(n - 1) // H] = quantise(x_grouped[(n - 1) // H], "x")
-            if H <= n + AHEAD < STEPS:
-                load_head(n + AHEAD)
-                if (n + AHEAD) % H == 0:
-                    load_x((n + AHEAD) // H)
-            if is_step(n):
-                e_done[n] = exponentials(n, s_done[n][0], s_done[n][1])
-            if is_step(n + 2):
-                qk_t[n + 2] = flip_q_and_k(n + 2)
-            if is_step(n + 1):
-                s_done[n + 1] = scores(qk_t[n + 1])
-            if is_step(n - 1):
-                e_grouped[n - 1] = flip(e_done[n - 1][0], "e")
-                v_grouped[n - 1] = regroup_values(project_values(n - 1, x_mx[(n - 1) // H], w_mx[0]))
-            if is_step(n - 2):
-                o_ps[n - 2] = attend(e_mx[n - 2], v_mx[n - 2])
-            if is_step(n) and n % H == 0:
-                if n == 0:
-                    x_grouped["wv"] = flip(wv_rows, "w")
-                x_grouped[n // H] = flip(x_of[n // H], "x")
+        def is_pair(n):
+            return 0 <= n < PAIRS
+
+        for n in range(-1, PAIRS + 2):
+            later = (n - 1) // H + 1
+            unit = (n - 1) % H
+            ready = 1 <= n and later < PAIRS // H
+            if is_pair(n + AHEAD) and n + AHEAD >= AHEAD:
+                for m in range(2):
+                    load_member(n + AHEAD, m)
+            if n >= 0 and n % H == 0 and n // H + 1 < PAIRS // H:
+                load_x(n // H + 1)
+            if is_pair(n):
+                scores(n, 1)
+            if is_pair(n - 1):
+                flip_e(n - 1, 1)
+            if n == 0:
+                flip_x((0, 0), x_of[0, 0], 0)
+                flip_x((0, 0), x_of[0, 0], 1)
+            if is_pair(n):
+                maxima(n, 0)
+            if is_pair(n - 2):
+                normalise(n - 2, 1)
+                store(n - 2, 1)
+            if is_pair(n - 1):
+                quantise_e(n - 1, 0)
+                exponentials(n - 1, 4)
+                copy_v(n - 1, 0)
+            if n == 0:
+                copy_x("wv", 0)
+                copy_x("wv", 1)
+            if is_pair(n):
+                scores(n, 2)
+            if is_pair(n - 1):
+                flip_e(n - 1, 2)
+            if n == 0:
+                flip_x((0, 1), x_of[0, 1], 0)
+                flip_x((0, 1), x_of[0, 1], 1)
+            if is_pair(n):
+                maxima(n, 1)
+            if n == 0:
+                quantise_x("wv")
+            if is_pair(n - 2):
+                normalise(n - 2, 0)
+                store(n - 2, 0)
+            if is_pair(n):
+                exponentials(n, 0)
+            if is_pair(n - 1):
+                copy_e(n - 1, 1)
+                copy_v(n - 1, 1)
+            if n == 0:
+                copy_x((0, 0), 0)
+                copy_x((0, 0), 1)
+            if is_pair(n):
+                scores(n, 3)
+            if ready:
+                flip_x((later, unit // 2), x_of[later, unit // 2], unit % 2)
+            if is_pair(n + 1):
+                flip_q_and_k(n + 1, 0)
+            if is_pair(n):
+                maxima(n, 2)
+            if n == 0:
+                quantise_x((0, 0))
+            if is_pair(n - 1):
+                quantise_v(n - 1)
+                quantise_e(n - 1, 1)
+                copy_halves(n - 1, 0)
+                copy_halves(n - 1, 1)
+                invert(n - 1)
+            if is_pair(n):
+                exponentials(n, 1)
+            if is_pair(n - 1):
+                copy_e(n - 1, 2)
+            if n == 0:
+                copy_x((0, 1), 0)
+                copy_x((0, 1), 1)
+            if is_pair(n):
+                scores(n, 4)
+                flip_e(n, 0)
+            if is_pair(n + 1):
+                flip_q_and_k(n + 1, 1)
+            if is_pair(n):
+                maxima(n, 3)
+            if is_pair(n + 1):
+                copy_q_and_k(n + 1, 0)
+            if n == 0:
+                quantise_x((0, 1))
+            if is_pair(n - 1):
+                quantise_e(n - 1, 2)
+            if is_pair(n):
+                exponentials(n, 2)
+            if ready:
+                copy_x((later, unit // 2), unit % 2)
+            if is_pair(n + 1):
+                scores(n + 1, 0)
+            if is_pair(n - 1):
+                attend_high(n - 1)
+                attend_low(n - 1)
+            if ready and unit % 2 == 1:
+                quantise_x((later, unit // 2))
+            if is_pair(n):
+                project_values(n, 0)
+                project_values(n, 1)
+            if n == -1:
+                flip_x("wv", wv_rows, 0)
+                flip_x("wv", wv_rows, 1)
+            if is_pair(n):
+                maxima(n, 4)
+            if is_pair(n + 1):
+                copy_q_and_k(n + 1, 1)
+            if is_pair(n):
+                exponentials(n, 3)
+                copy_e(n, 0)

@@ -25,7 +25,9 @@ MASKED = -1.0e30
 PAIRS = B * H // 2
 SEEN = [(i + 1) * P for i in range(TILES)]
 BANKS = [[(0, 3)], [(1, 3)], [(0, 2), (0, 0)], [(1, 2), (1, 0)], [(0, 1), (1, 1)]]
-GROUPS = [[(0, 3)], [(1, 3)], [(0, 2)], [(1, 2)], [(0, 1), (1, 1)], [(0, 0), (1, 0)]]
+GROUPS = [[(0, 3)], [(1, 3)], [(0, 2), (1, 0)], [(0, 0), (1, 2)], [(0, 1), (1, 1)]]
+SLOTS = [[(0, 0), (1, 2), (0, 3), (1, 3)], [(0, 1), (0, 2), (1, 0), (1, 1)]]
+SLOT_OF = {SLOTS[half][j]: 4 * half + j for half in range(2) for j in range(4)}
 GROUP_OF = {tile: g for g in range(len(GROUPS)) for tile in GROUPS[g]}
 AHEAD = 3
 
@@ -92,23 +94,20 @@ def tile_stridedattention_pa_t_kernel(tc, q, k, x, wv, out):
         nc.vector.memset(later_block[0:STRIDE, :], MASKED)
         nc.vector.memset(later_block[STRIDE:P, :], 0.0)
         e_buffers, r_buffers = [], []
-        for j in range(2):
+        for j in range(3):
             e_rows = const.tile([P, len(GROUPS), 2, 2 * P], BF16, name="e_rows%d" % j)
-            nc.vector.memset(e_rows[:, 2, :, 192:256], 0.0)
-            nc.vector.memset(e_rows[:, 3, :, 0:64], 0.0)
-            nc.vector.memset(e_rows[:, 5, :, 64:192], 0.0)
             e_buffers.append(e_rows)
-            halves = const.tile([P, 2 * HD], U32, align_bytes=64, name="halves%d" % j)
-            nc.vector.memset(halves[:].bitcast(I32), 0)
-            r_buffers.append(halves)
+            parts = const.tile([P, 3, 2 * HD], U32, align_bytes=64, name="parts%d" % j)
+            nc.vector.memset(parts[:].rearrange("p g c -> p (g c)").bitcast(I32), 0)
+            r_buffers.append(parts)
 
         def passing(shape, dtype):
             bank = psum.tile(shape, dtype, tag="passing", bufs=5)
             return bank
 
         def flip_words(words):
-            flipped = passing([P, 2, 2, P], F32)
-            for a in range(2):
+            flipped = passing([P, len(words) // 2, 2, P], F32)
+            for a in range(len(words) // 2):
                 for u in range(2):
                     nc.tensor.transpose(flipped[:, a, u, :], words[2 * a + u], ident_f32[:])
             return flipped
@@ -116,14 +115,14 @@ def tile_stridedattention_pa_t_kernel(tc, q, k, x, wv, out):
         def regroup(flipped, grouped, half):
             out_words = grouped[:].bitcast(F32).rearrange("p (a r u) -> p a r u", r=P, u=2)
             nc.scalar.copy(
-                out=out_words[:, 2 * half : 2 * half + 2, :, :],
+                out=out_words[:, 2 * half : 2 * half + flipped.shape[1], :, :],
                 in_=flipped[:].rearrange("p a u r -> p a r u"),
             )
 
         def quantise(grouped, what):
             width = grouped.shape[1] // PACK
-            codes = work.tile([P, width], U32, align_bytes=64, tag=what + "_codes")
-            scales = work.tile([P, width], U8, align_bytes=64, tag=what + "_scales")
+            codes = work.tile([P, width], U32, align_bytes=64, tag=what + "_codes", bufs=3)
+            scales = work.tile([P, width], U8, align_bytes=64, tag=what + "_scales", bufs=3)
             nc.vector.quantize_mx(out=codes[:].bitcast(FP8X4), scales=scales[:], in_=grouped[:])
             return codes, scales
 
@@ -210,16 +209,18 @@ def tile_stridedattention_pa_t_kernel(tc, q, k, x, wv, out):
                     out=target.rearrange("p u (w e) -> p u w e", e=2),
                     in_=s_ps[:, first : first + seen].rearrange("p (w u e) -> p u w e", u=2, e=2),
                     func=EXP, bias=bias[:, j : j + 1], scale=SCALE,
-                    accum_out=sums_of[n][:, 2 * i + m : 2 * i + m + 1],
+                    accum_out=sums_of[n][:, SLOT_OF[m, i] : SLOT_OF[m, i] + 1],
                 )
                 first += seen
 
         def flip_e(n, f):
             words = e_buffers[n % 2][:].rearrange("p g u c -> p (g u c)").bitcast(F32)
-            e_flipped[n, f] = flip_words([words[:, (4 * f + j) * P : (4 * f + j + 1) * P] for j in range(4)])
+            last = min(4 * f + 4, 2 * len(GROUPS))
+            e_flipped[n, f] = flip_words([words[:, j * P : (j + 1) * P] for j in range(4 * f, last)])
 
         def copy_e(n, f):
-            grouped = work.tile([P, 2 * P * PACK], BF16, align_bytes=64, tag="e_grouped", bufs=3)
+            columns = e_flipped[n, f].shape[1] * P
+            grouped = work.tile([P, columns * PACK], BF16, align_bytes=64, tag="e_grouped", bufs=3)
             regroup(e_flipped[n, f], grouped, 0)
             e_grouped[n, f] = grouped
 
@@ -267,68 +268,80 @@ def tile_stridedattention_pa_t_kernel(tc, q, k, x, wv, out):
         def quantise_v(n):
             v_mx[n] = quantise(v_grouped[n], "v")
 
-        def copy_halves(n, m):
-            rows = slice(m * P // 2, (m + 1) * P // 2)
-            cols = slice(m * HD, (m + 1) * HD)
-            nc.vector.tensor_copy(
-                out=r_buffers[n % 2][rows, cols].bitcast(I32), in_=v_mx[n][0][rows, cols].bitcast(I32)
-            )
+        def copy_parts(n):
+            for j in range(3):
+                border = [96, 32, 64][j]
+                for rows, m in ((slice(0, border), 0), (slice(border, P), 1)):
+                    cols = slice(m * HD, (m + 1) * HD)
+                    nc.sync.dma_start(
+                        out=r_buffers[n % 3][rows, j, cols].bitcast(I32), in_=v_mx[n][0][rows, cols].bitcast(I32)
+                    )
 
-        def attend(n, group, bank, first, width, codes, member):
+        def attend(n, group, bank, slot, codes, scales):
             e_codes, e_scales = e_mx[n, group // 2]
             cols = slice((group % 2) * P, (group % 2 + 1) * P)
+            first = (slot % 4) * HD
             nc.tensor.matmul_mx(
-                out=bank[:, first : first + width],
+                out=bank[:, first : first + codes.shape[1]],
                 lhsT=e_codes[:, cols].bitcast(FP8X4),
                 lhsT_scale=e_scales[:, cols],
-                rhs=codes[:, member * HD : member * HD + width].bitcast(FP8X4),
-                rhs_scale=v_mx[n][1][:, member * HD : member * HD + width],
+                rhs=codes.bitcast(FP8X4),
+                rhs_scale=scales,
                 start=True,
                 stop=True,
             )
 
-        def attend_high(n):
+        def attend_first(n):
             bank = passing([P, 4 * HD], F32)
-            for j in range(4):
-                group = (2 + j) % 4
-                attend(n, group, bank, j * HD, HD, v_mx[n][0], j % 2)
-            o_ps[n, 1] = bank
-
-        def attend_low(n):
-            bank = passing([P, 4 * HD], F32)
-            for j in range(2):
-                attend(n, 5 - j, bank, 2 * j * HD, 2 * HD, r_buffers[n % 2], 0)
+            codes, scales = v_mx[n]
+            for m in range(2):
+                cols = slice(m * HD, (m + 1) * HD)
+                attend(n, m, bank, 2 + m, codes[:, cols], scales[:, cols])
+            attend(n, 3, bank, 0, r_buffers[n % 3][:, 1, :], scales[:])
             o_ps[n, 0] = bank
 
+        def attend_second(n):
+            bank = passing([P, 4 * HD], F32)
+            scales = v_mx[n][1]
+            attend(n, 2, bank, 5, r_buffers[n % 3][:, 0, :], scales[:])
+            for m in range(2):
+                cols = slice(m * HD, (m + 1) * HD)
+                attend(n, 4, bank, 4 + 3 * m, r_buffers[n % 3][:, 2, cols], scales[:, cols])
+            o_ps[n, 1] = bank
+
         def invert(n):
-            inv = work.tile([P, 2 * TILES], F32, tag="inv_sum")
+            inv = work.tile([P, 2 * TILES], F32, tag="inv_sum", bufs=4)
             nc.vector.reciprocal(out=inv[:], in_=sums_of[n][:])
             inv_of[n] = inv
 
-        def normalise(n, high):
-            if high:
+        def normalise(n, half):
+            if half == 0:
                 o_sb = work.tile([P, 2 * TILES, HD], F32, tag="o_sb", bufs=3)
                 o_of[n] = o_sb
-            slots = slice(4 * high, 4 * high + 4)
+            slots = slice(4 * half, 4 * half + 4)
             nc.vector.tensor_tensor(
                 out=o_of[n][:, slots, :],
-                in0=o_ps[n, high][:].rearrange("p (s f) -> p s f", f=HD),
+                in0=o_ps[n, half][:].rearrange("p (s f) -> p s f", f=HD),
                 in1=inv_of[n][:, slots].unsqueeze(2).to_broadcast([P, 4, HD]),
                 op=MULT,
             )
 
-        def store(n, high):
+        def store(n, half):
             for m in range(2):
                 b, h = place(n, m)
+                tiles = [i for member, i in SLOTS[half] if member == m]
+                slots = [SLOT_OF[m, i] for i in tiles]
                 nc.sync.dma_start(
-                    out=out[b].rearrange("(i p) c -> p i c", p=P)[:, 2 * high : 2 * high + 2, h * HD : (h + 1) * HD],
-                    in_=o_of[n][:].rearrange("p (i m) f -> p i m f", m=2)[:, 2 * high : 2 * high + 2, m, :],
+                    out=out[b].rearrange("(i p) c -> p i c", p=P)[
+                        :, tiles[0] : tiles[1] + 1 : tiles[1] - tiles[0], h * HD : (h + 1) * HD
+                    ],
+                    in_=o_of[n][:, slots[0] : slots[1] + 1 : slots[1] - slots[0], :],
                 )
 
         def is_pair(n):
             return 0 <= n < PAIRS
 
-        for n in range(-1, PAIRS + 2):
+        for n in range(-1, PAIRS + 3):
             later = (n - 1) // H + 1
             unit = (n - 1) % H
             ready = 1 <= n and later < PAIRS // H
@@ -346,9 +359,9 @@ def tile_stridedattention_pa_t_kernel(tc, q, k, x, wv, out):
                 flip_x((0, 0), x_of[0, 0], 1)
             if is_pair(n):
                 maxima(n, 0)
-            if is_pair(n - 2):
-                normalise(n - 2, 1)
-                store(n - 2, 1)
+            if is_pair(n - 3):
+                normalise(n - 3, 0)
+                store(n - 3, 0)
             if is_pair(n - 1):
                 quantise_e(n - 1, 0)
                 exponentials(n - 1, 4)
@@ -367,14 +380,14 @@ def tile_stridedattention_pa_t_kernel(tc, q, k, x, wv, out):
                 maxima(n, 1)
             if n == 0:
                 quantise_x("wv")
-            if is_pair(n - 2):
-                normalise(n - 2, 0)
-                store(n - 2, 0)
+            if is_pair(n - 3):
+                normalise(n - 3, 1)
+                store(n - 3, 1)
             if is_pair(n):
                 exponentials(n, 0)
             if is_pair(n - 1):
-                copy_e(n - 1, 1)
                 copy_v(n - 1, 1)
+                copy_e(n - 1, 1)
             if n == 0:
                 copy_x((0, 0), 0)
                 copy_x((0, 0), 1)
@@ -390,9 +403,7 @@ def tile_stridedattention_pa_t_kernel(tc, q, k, x, wv, out):
                 quantise_x((0, 0))
             if is_pair(n - 1):
                 quantise_v(n - 1)
-                quantise_e(n - 1, 1)
-                copy_halves(n - 1, 0)
-                copy_halves(n - 1, 1)
+                copy_parts(n - 1)
                 invert(n - 1)
             if is_pair(n):
                 exponentials(n, 1)
@@ -408,26 +419,23 @@ def tile_stridedattention_pa_t_kernel(tc, q, k, x, wv, out):
                 flip_q_and_k(n + 1, 1)
             if is_pair(n):
                 maxima(n, 3)
+            if is_pair(n - 1):
+                quantise_e(n - 1, 1)
             if is_pair(n + 1):
                 copy_q_and_k(n + 1, 0)
             if n == 0:
                 quantise_x((0, 1))
-            if is_pair(n - 1):
-                quantise_e(n - 1, 2)
             if is_pair(n):
                 exponentials(n, 2)
             if ready:
                 copy_x((later, unit // 2), unit % 2)
             if is_pair(n + 1):
                 scores(n + 1, 0)
-            if is_pair(n - 1):
-                attend_high(n - 1)
-                attend_low(n - 1)
-            if ready and unit % 2 == 1:
-                quantise_x((later, unit // 2))
             if is_pair(n):
                 project_values(n, 0)
-                project_values(n, 1)
+            if is_pair(n - 2):
+                attend_first(n - 2)
+                attend_second(n - 2)
             if n == -1:
                 flip_x("wv", wv_rows, 0)
                 flip_x("wv", wv_rows, 1)
@@ -435,6 +443,12 @@ def tile_stridedattention_pa_t_kernel(tc, q, k, x, wv, out):
                 maxima(n, 4)
             if is_pair(n + 1):
                 copy_q_and_k(n + 1, 1)
+            if ready and unit % 2 == 1:
+                quantise_x((later, unit // 2))
+            if is_pair(n - 1):
+                quantise_e(n - 1, 2)
+            if is_pair(n):
+                project_values(n, 1)
             if is_pair(n):
                 exponentials(n, 3)
                 copy_e(n, 0)

from contextlib import ExitStack

import concourse.mybir as mybir
from concourse.masks import make_identity

BF16 = mybir.dt.bfloat16
F32 = mybir.dt.float32
I32 = mybir.dt.int32
U32 = mybir.dt.uint32
U8 = mybir.dt.uint8
FP8X4 = mybir.dt.float8_e4m3fn_x4
EXP = mybir.ActivationFunctionType.Exp
MULT = mybir.AluOpType.mult
ADD = mybir.AluOpType.add
MAX = mybir.AluOpType.max
AXIS_X = mybir.AxisListType.X

B, T, D, H, HD = 8, 512, 512, 4, 128
STRIDE = 64
P = 128
PACK = 4
TILES = T // P
SCALE = HD**-0.5
MASKED = -1.0e30
PAIRS = B * H // 2
SEEN = [(i + 1) * P for i in range(TILES)]
BANKS = [[(0, 3)], [(1, 3)], [(0, 2), (0, 0)], [(1, 2), (1, 0)], [(0, 1), (1, 1)]]
GROUPS = [[(0, 3)], [(1, 3)], [(0, 2), (1, 0)], [(0, 0), (1, 2)], [(0, 1), (1, 1)]]
SLOTS = [[(0, 0), (1, 2), (0, 3), (1, 3)], [(0, 1), (0, 2), (1, 0), (1, 1)]]
SLOT_OF = {SLOTS[half][j]: 4 * half + j for half in range(2) for j in range(4)}
GROUP_OF = {tile: g for g in range(len(GROUPS)) for tile in GROUPS[g]}
AHEAD = 3

FLOPS = 2 * B * T * D * D + 2 * 2 * B * H * T * T * HD


def tile_stridedattention_pa_t_kernel(tc, q, k, x, wv, out):
    nc = tc.nc
    with ExitStack() as ctx:
        const = ctx.enter_context(tc.tile_pool(name="const", bufs=1))
        loads = ctx.enter_context(tc.tile_pool(name="loads", bufs=8))
        work = ctx.enter_context(tc.tile_pool(name="work", bufs=2))
        psum = ctx.enter_context(tc.psum_pool(name="psum", bufs=1))
        ctx.enter_context(tc.manual_schedule())

        def place(n, m):
            return 2 * (n // H) + m, n % H

        q_of, k_of, x_of = {}, {}, {}

        def load_member(n, m):
            b, h = place(n, m)
            q_rows = loads.tile([P, TILES * HD], BF16)
            nc.sync.dma_start(
                out=q_rows[:].rearrange("p (i d) -> p i d", d=HD),
                in_=q[b][h].rearrange("(i p) d -> p i d", p=P),
            )
            k_rows = loads.tile([P, TILES * HD], BF16)
            nc.sync.dma_start(
                out=k_rows[:].rearrange("p (i d) -> p i d", d=HD),
                in_=k[b][h].rearrange("(i p) d -> p i d", p=P),
            )
            q_of[n, m], k_of[n, m] = q_rows, k_rows

        def load_x(bp):
            x_0 = loads.tile([P, TILES * D], BF16, bufs=2)
            nc.sync.dma_start(out=x_0[:], in_=x[2 * bp].rearrange("(p a) c -> p (a c)", a=PACK))
            x_1 = loads.tile([P, TILES * D], BF16, bufs=2)
            for quarter in range(TILES):
                block = TILES - 1 - quarter
                nc.sync.dma_start(
                    out=x_1[32 * quarter : 32 * (quarter + 1), :],
                    in_=x[2 * bp + 1][block * P : (block + 1) * P, :].rearrange("(p a) c -> p (a c)", a=PACK),
                )
            x_of[bp, 0], x_of[bp, 1] = x_0, x_1

        load_member(0, 0)
        load_member(0, 1)
        wv_rows = const.tile([P, TILES * D], BF16)
        nc.sync.dma_start(
            out=wv_rows[:].rearrange("p (a c) -> p a c", a=TILES),
            in_=wv.rearrange("(a p) c -> p a c", p=P),
        )
        load_x(0)
        for n in range(1, AHEAD):
            for m in range(2):
                load_member(n, m)

        ident_bf = const.tile([P, P], BF16)
        make_identity(nc, ident_bf[:])
        ident_f32 = const.tile([P, P], F32)
        make_identity(nc, ident_f32[:])
        later_block = const.tile([P, STRIDE], BF16)
        nc.vector.memset(later_block[0:STRIDE, :], MASKED)
        nc.vector.memset(later_block[STRIDE:P, :], 0.0)
        e_buffers, r_buffers = [], []
        for j in range(3):
            e_rows = const.tile([P, len(GROUPS), 2, 2 * P], BF16, name="e_rows%d" % j)
            e_buffers.append(e_rows)
            parts = const.tile([P, 3, 2 * HD], U32, align_bytes=64, name="parts%d" % j)
            nc.vector.memset(parts[:].rearrange("p g c -> p (g c)").bitcast(I32), 0)
            r_buffers.append(parts)

        def passing(shape, dtype):
            bank = psum.tile(shape, dtype, tag="passing", bufs=5)
            return bank

        def flip_words(words):
            flipped = passing([P, len(words) // 2, 2, P], F32)
            for a in range(len(words) // 2):
                for u in range(2):
                    nc.tensor.transpose(flipped[:, a, u, :], words[2 * a + u], ident_f32[:])
            return flipped

        def regroup(flipped, grouped, half):
            out_words = grouped[:].bitcast(F32).rearrange("p (a r u) -> p a r u", r=P, u=2)
            nc.scalar.copy(
                out=out_words[:, 2 * half : 2 * half + flipped.shape[1], :, :],
                in_=flipped[:].rearrange("p a u r -> p a r u"),
            )

        def quantise(grouped, what):
            width = grouped.shape[1] // PACK
            codes = work.tile([P, width], U32, align_bytes=64, tag=what + "_codes", bufs=3)
            scales = work.tile([P, width], U8, align_bytes=64, tag=what + "_scales", bufs=3)
            nc.vector.quantize_mx(out=codes[:].bitcast(FP8X4), scales=scales[:], in_=grouped[:])
            return codes, scales

        def feature_words(rows, half):
            words = rows[:].bitcast(F32)
            return [words[:, (4 * half + j) * P : (4 * half + j + 1) * P] for j in range(4)]

        qk_t, s_of, bias_of, sums_of = {}, {}, {}, {}
        e_flipped, e_grouped, e_mx = {}, {}, {}
        x_flipped, x_grouped, x_mx = {}, {}, {}
        v_ps, v_grouped, v_mx, halves_of = {}, {}, {}, {}
        o_ps, inv_of, o_of = {}, {}, {}
        qk_ps = {}

        def flip_q_and_k(n, m):
            both = passing([P, 2 * T], BF16)
            for i in range(TILES):
                rows = slice(i * HD, (i + 1) * HD)
                key_block = i if m == 0 else TILES - 1 - i
                nc.tensor.transpose(both[:, i * P : (i + 1) * P], q_of[n, m][:, rows], ident_bf[:])
                nc.tensor.transpose(
                    both[:, T + key_block * P : T + (key_block + 1) * P], k_of[n, m][:, rows], ident_bf[:]
                )
            qk_ps[n, m] = both

        def copy_q_and_k(n, m):
            copied = work.tile([P, 2 * T], BF16, tag="qk_t%d" % m)
            nc.vector.tensor_copy(out=copied[:], in_=qk_ps[n, m][:])
            qk_t[n, m] = copied

        def scores(n, bank):
            s_ps = psum.tile([P, T], F32, tag="scores", bufs=3)
            first = 0
            for m, i in BANKS[bank]:
                s_tile = s_ps[:, first : first + SEEN[i]]
                keys = T if m == 0 else 2 * T - SEEN[i]
                nc.tensor.matmul(
                    s_tile, lhsT=qk_t[n, m][:, i * P : (i + 1) * P], rhs=qk_t[n, m][:, keys : keys + SEEN[i]],
                    start=True, stop=False,
                )
                later = SEEN[i] - STRIDE if m == 0 else STRIDE
                nc.tensor.matmul(
                    s_tile[:, later : later + STRIDE], lhsT=ident_bf[:], rhs=later_block[:],
                    start=False, stop=True,
                )
                first += SEEN[i]
            s_of[n, bank] = s_ps

        def maxima(n, bank):
            tiles = BANKS[bank]
            s_ps = s_of[n, bank]
            row_max = work.tile([P, 2], F32, tag="row_max", bufs=4)
            if bank == 4:
                nc.vector.tensor_reduce(
                    out=row_max[:], in_=s_ps[:].rearrange("p (j c) -> p j c", j=2), axis=AXIS_X, op=MAX
                )
            else:
                first = 0
                for j in range(len(tiles)):
                    seen = SEEN[tiles[j][1]]
                    nc.vector.tensor_reduce(
                        out=row_max[:, j : j + 1], in_=s_ps[:, first : first + seen], axis=AXIS_X, op=MAX
                    )
                    first += seen
            bias = work.tile([P, 2], F32, tag="bias", bufs=4)
            used = len(tiles)
            nc.gpsimd.tensor_scalar(
                out=bias[:, :used], in0=row_max[:, :used], scalar1=-SCALE, scalar2=0.0, op0=MULT, op1=ADD
            )
            bias_of[n, bank] = bias

        def exponentials(n, bank):
            s_ps, bias = s_of[n, bank], bias_of[n, bank]
            if bank == 0:
                row_sum = work.tile([P, 2 * TILES], F32, tag="row_sum", bufs=3)
                sums_of[n] = row_sum
            first = 0
            for j in range(len(BANKS[bank])):
                m, i = BANKS[bank][j]
                seen = SEEN[i]
                start = 0 if m == 0 else (T - seen) // 2
                target = e_buffers[n % 2][:, GROUP_OF[m, i], :, start : start + seen // 2]
                nc.scalar.activation(
                    out=target.rearrange("p u (w e) -> p u w e", e=2),
                    in_=s_ps[:, first : first + seen].rearrange("p (w u e) -> p u w e", u=2, e=2),
                    func=EXP, bias=bias[:, j : j + 1], scale=SCALE,
                    accum_out=sums_of[n][:, SLOT_OF[m, i] : SLOT_OF[m, i] + 1],
                )
                first += seen

        def flip_e(n, f):
            words = e_buffers[n % 2][:].rearrange("p g u c -> p (g u c)").bitcast(F32)
            last = min(4 * f + 4, 2 * len(GROUPS))
            e_flipped[n, f] = flip_words([words[:, j * P : (j + 1) * P] for j in range(4 * f, last)])

        def copy_e(n, f):
            columns = e_flipped[n, f].shape[1] * P
            grouped = work.tile([P, columns * PACK], BF16, align_bytes=64, tag="e_grouped", bufs=3)
            regroup(e_flipped[n, f], grouped, 0)
            e_grouped[n, f] = grouped

        def quantise_e(n, f):
            e_mx[n, f] = quantise(e_grouped[n, f], "e%d" % f)

        def flip_x(key, rows, half):
            x_flipped[key, half] = flip_words(feature_words(rows, half))

        def copy_x(key, half):
            if half == 0:
                grouped = work.tile([P, TILES * P * PACK], BF16, align_bytes=64, tag="x_grouped")
                x_grouped[key] = grouped
            regroup(x_flipped[key, half], x_grouped[key], half)

        def quantise_x(key):
            x_mx[key] = quantise(x_grouped[key], "w" if key == "wv" else "x%d" % key[1])

        def project_values(n, m):
            bp, h = n // H, n % H
            codes, scales = x_mx[bp, m]
            w_codes, w_scales = x_mx["wv"]
            bank = passing([P, PACK, HD], F32)
            for a in range(PACK):
                nc.tensor.matmul_mx(
                    out=bank[:, a, :],
                    lhsT=codes[:, a * P : (a + 1) * P].bitcast(FP8X4),
                    lhsT_scale=scales[:, a * P : (a + 1) * P],
                    rhs=w_codes[:, h * HD : (h + 1) * HD].bitcast(FP8X4),
                    rhs_scale=w_scales[:, h * HD : (h + 1) * HD],
                    start=True,
                    stop=True,
                )
            v_ps[n, m] = bank

        def copy_v(n, m):
            if m == 0:
                grouped = work.tile([P, 2 * HD * PACK], BF16, align_bytes=64, tag="v_grouped")
                v_grouped[n] = grouped
            nc.scalar.copy(
                out=v_grouped[n][:, m * HD * PACK : (m + 1) * HD * PACK].rearrange("p (f a) -> p f a", a=PACK),
                in_=v_ps[n, m][:].rearrange("p a f -> p f a"),
            )

        def quantise_v(n):
            v_mx[n] = quantise(v_grouped[n], "v")

        def copy_parts(n):
            for j in range(3):
                border = [96, 32, 64][j]
                for rows, m in ((slice(0, border), 0), (slice(border, P), 1)):
                    cols = slice(m * HD, (m + 1) * HD)
                    nc.sync.dma_start(
                        out=r_buffers[n % 3][rows, j, cols].bitcast(I32), in_=v_mx[n][0][rows, cols].bitcast(I32)
                    )

        def attend(n, group, bank, slot, codes, scales):
            e_codes, e_scales = e_mx[n, group // 2]
            cols = slice((group % 2) * P, (group % 2 + 1) * P)
            first = (slot % 4) * HD
            nc.tensor.matmul_mx(
                out=bank[:, first : first + codes.shape[1]],
                lhsT=e_codes[:, cols].bitcast(FP8X4),
                lhsT_scale=e_scales[:, cols],
                rhs=codes.bitcast(FP8X4),
                rhs_scale=scales,
                start=True,
                stop=True,
            )

        def attend_first(n):
            bank = passing([P, 4 * HD], F32)
            codes, scales = v_mx[n]
            for m in range(2):
                cols = slice(m * HD, (m + 1) * HD)
                attend(n, m, bank, 2 + m, codes[:, cols], scales[:, cols])
            attend(n, 3, bank, 0, r_buffers[n % 3][:, 1, :], scales[:])
            o_ps[n, 0] = bank

        def attend_second(n):
            bank = passing([P, 4 * HD], F32)
            scales = v_mx[n][1]
            attend(n, 2, bank, 5, r_buffers[n % 3][:, 0, :], scales[:])
            for m in range(2):
                cols = slice(m * HD, (m + 1) * HD)
                attend(n, 4, bank, 4 + 3 * m, r_buffers[n % 3][:, 2, cols], scales[:, cols])
            o_ps[n, 1] = bank

        def invert(n):
            inv = work.tile([P, 2 * TILES], F32, tag="inv_sum", bufs=4)
            nc.vector.reciprocal(out=inv[:], in_=sums_of[n][:])
            inv_of[n] = inv

        def normalise(n, half):
            if half == 0:
                o_sb = work.tile([P, 2 * TILES, HD], F32, tag="o_sb", bufs=3)
                o_of[n] = o_sb
            slots = slice(4 * half, 4 * half + 4)
            nc.vector.tensor_tensor(
                out=o_of[n][:, slots, :],
                in0=o_ps[n, half][:].rearrange("p (s f) -> p s f", f=HD),
                in1=inv_of[n][:, slots].unsqueeze(2).to_broadcast([P, 4, HD]),
                op=MULT,
            )

        def store(n, half):
            for m in range(2):
                b, h = place(n, m)
                tiles = [i for member, i in SLOTS[half] if member == m]
                slots = [SLOT_OF[m, i] for i in tiles]
                nc.sync.dma_start(
                    out=out[b].rearrange("(i p) c -> p i c", p=P)[
                        :, tiles[0] : tiles[1] + 1 : tiles[1] - tiles[0], h * HD : (h + 1) * HD
                    ],
                    in_=o_of[n][:, slots[0] : slots[1] + 1 : slots[1] - slots[0], :],
                )

        def is_pair(n):
            return 0 <= n < PAIRS

        for n in range(-1, PAIRS + 3):
            later = (n - 1) // H + 1
            unit = (n - 1) % H
            ready = 1 <= n and later < PAIRS // H
            if is_pair(n + AHEAD) and n + AHEAD >= AHEAD:
                for m in range(2):
                    load_member(n + AHEAD, m)
            if n >= 0 and n % H == 0 and n // H + 1 < PAIRS // H:
                load_x(n // H + 1)
            if is_pair(n):
                scores(n, 1)
            if is_pair(n - 1):
                flip_e(n - 1, 1)
            if n == 0:
                flip_x((0, 0), x_of[0, 0], 0)
                flip_x((0, 0), x_of[0, 0], 1)
            if is_pair(n):
                maxima(n, 0)
            if is_pair(n - 3):
                normalise(n - 3, 0)
                store(n - 3, 0)
            if is_pair(n - 1):
                quantise_e(n - 1, 0)
                exponentials(n - 1, 4)
                copy_v(n - 1, 0)
            if n == 0:
                copy_x("wv", 0)
                copy_x("wv", 1)
            if is_pair(n):
                scores(n, 2)
            if is_pair(n - 1):
                flip_e(n - 1, 2)
            if n == 0:
                flip_x((0, 1), x_of[0, 1], 0)
                flip_x((0, 1), x_of[0, 1], 1)
            if is_pair(n):
                maxima(n, 1)
            if n == 0:
                quantise_x("wv")
            if is_pair(n - 3):
                normalise(n - 3, 1)
                store(n - 3, 1)
            if is_pair(n):
                exponentials(n, 0)
            if is_pair(n - 1):
                copy_v(n - 1, 1)
                copy_e(n - 1, 1)
            if n == 0:
                copy_x((0, 0), 0)
                copy_x((0, 0), 1)
            if is_pair(n):
                scores(n, 3)
            if ready:
                flip_x((later, unit // 2), x_of[later, unit // 2], unit % 2)
            if is_pair(n + 1):
                flip_q_and_k(n + 1, 0)
            if is_pair(n):
                maxima(n, 2)
            if n == 0:
                quantise_x((0, 0))
            if is_pair(n - 1):
                quantise_v(n - 1)
                copy_parts(n - 1)
                invert(n - 1)
            if is_pair(n):
                exponentials(n, 1)
            if is_pair(n - 1):
                copy_e(n - 1, 2)
            if n == 0:
                copy_x((0, 1), 0)
                copy_x((0, 1), 1)
            if is_pair(n):
                scores(n, 4)
                flip_e(n, 0)
            if is_pair(n + 1):
                flip_q_and_k(n + 1, 1)
            if is_pair(n):
                maxima(n, 3)
            if is_pair(n - 1):
                quantise_e(n - 1, 1)
            if is_pair(n + 1):
                copy_q_and_k(n + 1, 0)
            if n == 0:
                quantise_x((0, 1))
            if is_pair(n):
                exponentials(n, 2)
            if ready:
                copy_x((later, unit // 2), unit % 2)
            if is_pair(n + 1):
                scores(n + 1, 0)
            if is_pair(n):
                project_values(n, 0)
            if is_pair(n - 2):
                attend_first(n - 2)
                attend_second(n - 2)
            if n == -1:
                flip_x("wv", wv_rows, 0)
                flip_x("wv", wv_rows, 1)
            if is_pair(n):
                maxima(n, 4)
            if is_pair(n + 1):
                copy_q_and_k(n + 1, 1)
            if ready and unit % 2 == 1:
                quantise_x((later, unit // 2))
            if is_pair(n - 1):
                quantise_e(n - 1, 2)
            if is_pair(n):
                project_values(n, 1)
            if is_pair(n):
                exponentials(n, 3)
                copy_e(n, 0)
